import numpy as np
import ml_dtypes


BF16 = ml_dtypes.bfloat16


def bf(x):
    return np.asarray(x, np.float32).astype(BF16)


def f64(x):
    return np.asarray(x).astype(np.float64)


E2M1 = np.array([0.0, 0.5, 1.0, 1.5, 2.0, 3.0, 4.0, 6.0, -0.0, -0.5, -1.0, -1.5, -2.0, -3.0, -4.0, -6.0])


def pack_weight(w, fmt):
    k, n = w.shape
    w = f64(bf(w)).reshape(k // 32, 32, n)
    amax = np.abs(w).max(1)
    if fmt == "e4m3":
        byte = np.frexp(amax)[1] - 1 + 127 - 7
    else:
        mant, ex = np.frexp(amax / 6.0)
        byte = np.where(mant > 0.5, ex, ex - 1) + 127
    byte = np.clip(np.where(amax > 0, byte, 1), 1, 254)
    scaled = (w * np.exp2(127.0 - byte)[:, None, :]).reshape(k, n).astype(np.float32)
    by_word = np.ascontiguousarray(scaled.reshape(k // 512, 128, 4, n).transpose(0, 1, 3, 2))
    if fmt == "e4m3":
        words = by_word.astype(ml_dtypes.float8_e4m3fn).view(np.uint8)
    else:
        c = by_word.astype(ml_dtypes.float4_e2m1fn).view(np.uint8) & 0xF
        words = c[..., 0::2] | (c[..., 1::2] << 4)
    return np.ascontiguousarray(words), np.ascontiguousarray(byte.astype(np.uint8).reshape(k // 512, 16, n))


def unpack_weight(words, scales, fmt):
    g, p, n, _ = words.shape
    if fmt == "e4m3":
        vals = np.ascontiguousarray(words).view(ml_dtypes.float8_e4m3fn).astype(np.float64)
    else:
        nib = np.empty((g, p, n, 4), np.uint8)
        nib[..., 0::2] = words & 0xF
        nib[..., 1::2] = words >> 4
        vals = E2M1[nib]
    vals = vals * np.repeat(np.exp2(scales.astype(np.float64) - 127.0), 8, axis=1)[..., None]
    return vals.transpose(0, 1, 3, 2).reshape(g * 512, n)

def pack4(w):
    words, scales = pack_weight(w, "e2m1")
    return words.reshape(words.shape[0], 128, -1), scales


def unpack4(words, scales):
    return unpack_weight(words.reshape(words.shape[0], 128, -1, 2), scales, "e2m1")


def kspread(k):
    return np.exp2(np.repeat(np.random.randint(-6, 7, k // 32), 32).astype(np.float64))


B, S, IN, OUT, A, R = 8, 128, 8192, 512, 8, 128
G = B // A
SCALING = 2.0


def setup_inputs():
    s = kspread(IN)
    data = np.random.standard_normal((B, S, IN)) * s
    data_words, data_scales = pack4(np.ascontiguousarray(data.reshape(B * S, IN).T))
    w = np.random.standard_normal((OUT, IN)) / np.sqrt(IN) / s
    W_words, W_scales = pack4(np.ascontiguousarray(w.T))
    t_lora = bf(np.random.standard_normal((A, G, S, R)))
    lora_b = bf(np.random.standard_normal((A, OUT, R)) * 0.5 / np.sqrt(R))
    return {"data_words": data_words,
            "data_scales": data_scales,
            "W_words": W_words,
            "W_scales": W_scales,
            "t_lora": t_lora,
            "lora_b": lora_b}


def reference(data_words, data_scales, W_words, W_scales, t_lora, lora_b):
    base = unpack4(data_words, data_scales).T.reshape(B, S, IN) @ unpack4(W_words, W_scales)
    delta = (f64(t_lora).reshape(A, G * S, R) @ f64(lora_b).transpose(0, 2, 1)) * SCALING
    return base + delta.reshape(B, S, OUT)

@@ -1,0 +1,183 @@
+from contextlib import ExitStack
+
+import concourse.mybir as mybir
+from concourse.masks import make_identity
+
+F32 = mybir.dt.float32
+BF16 = mybir.dt.bfloat16
+U8 = mybir.dt.uint8
+I32 = mybir.dt.int32
+FP4 = mybir.dt.float4_e2m1fn_x4
+COPY = mybir.ActivationFunctionType.Copy
+ADD = mybir.AluOpType.add
+
+P = 128
+PASSES = 16
+BLOCKS = 8
+OUT = 512
+RANK = 128
+TOKENS = 1024
+FLOPS = 2 * TOKENS * OUT * 8192 + 2 * TOKENS * OUT * RANK
+
+N_WARM = 5
+G1 = 10
+SCALE_RUNS = ((0, 2), (2, 6), (6, 10), (10, 16))
+B_CHUNKS = ((0, 1), (1, 4), (4, 8))
+EARLY_RUNS = 2
+
+
+def tile_linear_pa_kernel(tc, data_words, data_scales, W_words, W_scales, t_lora, lora_b, out):
+    nc = tc.nc
+    with ExitStack() as ctx:
+        keep = ctx.enter_context(tc.tile_pool(name="keep", bufs=1))
+        psum = ctx.enter_context(tc.psum_pool(name="psum", bufs=1))
+        ctx.enter_context(tc.manual_schedule())
+
+        def bank(i, dtype, name):
+            return psum.tile([P, 512], dtype, tag="bank%d" % i, name=name)
+
+        def sb(shape, dtype, name):
+            return keep.tile(shape, dtype, tag=name, name=name, align_bytes=64)
+
+        warm = sb([P, 512], BF16, "warm")
+        nc.vector.memset(warm[:], 0.0)
+        ident = sb([P, P], BF16, "ident")
+        make_identity(nc, ident[:])
+
+        b_raw = {}
+        t_raw = sb([P, BLOCKS, RANK], BF16, "t_raw")
+
+        def load_b(c):
+            a0, a1 = B_CHUNKS[c]
+            raw = sb([P, a1 - a0, 4 * RANK], BF16, "b_raw%d" % c)
+            nc.sync.dma_start(out=raw[:], in_=lora_b[a0:a1].rearrange("a (p j) r -> p a (j r)", j=4))
+            for a in range(a0, a1):
+                b_raw[a] = raw[:, a - a0, :]
+
+        load_b(0)
+        nc.sync.dma_start(out=t_raw[:], in_=t_lora.rearrange("a g s r -> s (a g) r"))
+        load_b(1)
+        load_b(2)
+
+        d_plane = {}
+        w_plane = {}
+        d_code = {}
+        w_code = {}
+
+        def load_run(r):
+            g0, g1 = SCALE_RUNS[r]
+            dpl = sb([P, g1 - g0, TOKENS], U8, "dpl%d" % r)
+            wpl = sb([P, g1 - g0, OUT], U8, "wpl%d" % r)
+            nc.vector.memset(dpl[:].bitcast(I32), 0)
+            nc.vector.memset(wpl[:].bitcast(I32), 0)
+            for q in range(4):
+                nc.sync.dma_start(
+                    out=wpl[32 * q : 32 * q + 4, :, :].bitcast(I32),
+                    in_=W_scales[g0:g1, 4 * q : 4 * q + 4, :].rearrange("g r n -> r g n").bitcast(I32),
+                )
+                nc.sync.dma_start(
+                    out=dpl[32 * q : 32 * q + 4, :, :].bitcast(I32),
+                    in_=data_scales[g0:g1, 4 * q : 4 * q + 4, :].rearrange("g r n -> r g n").bitcast(I32),
+                )
+            for g in range(g0, g1):
+                d_plane[g] = dpl[:, g - g0, :]
+                w_plane[g] = wpl[:, g - g0, :]
+            for g in range(g0, g1, 2):
+                wc = sb([P, 2, 2 * OUT], U8, "wc%d" % g)
+                nc.sync.dma_start(
+                    out=wc[:].bitcast(I32),
+                    in_=W_words[g : g + 2].rearrange("g p n -> p g n").bitcast(I32),
+                )
+                for h in (g, g + 1):
+                    w_code[h] = wc[:, h - g, :]
+                    dc = sb([P, 2 * TOKENS], U8, "dc%d" % h)
+                    nc.sync.dma_start(out=dc[:].bitcast(I32), in_=data_words[h].bitcast(I32))
+                    d_code[h] = dc
+
+        for r in range(EARLY_RUNS):
+            load_run(r)
+
+        scr = sb([P, 1], F32, "scr")
+        nc.scalar.activation(out=scr[:], in_=warm[:, 0:1], func=COPY, scale=2.0)
+        wps = bank(7, F32, "wps")
+        for i in range(N_WARM):
+            nc.tensor.matmul(out=wps[:], lhsT=warm[:, 0:P], rhs=warm[:], start=True, stop=True)
+
+        bT = {}
+
+        def transpose_b(a):
+            ps = bank(a % 3, BF16, "bTp%d" % a)
+            for j in range(4):
+                nc.tensor.transpose(out=ps[:, P * j : P * (j + 1)], in_=b_raw[a][:, P * j : P * (j + 1)], identity=ident[:])
+            bT[a] = sb([P, 512], BF16, "bT%d" % a)
+            nc.vector.tensor_copy(out=bT[a][:], in_=ps[:])
+
+        tT = []
+
+        def transpose_t(h):
+            ps = bank(3 + h, BF16, "tTp%d" % h)
+            for j in range(4):
+                nc.tensor.transpose(out=ps[:, P * j : P * (j + 1)], in_=t_raw[:, 4 * h + j, :], identity=ident[:])
+            tT.append(sb([P, 512], BF16, "tT%d" % h))
+            if h == 0:
+                nc.vector.tensor_copy(out=tT[h][:], in_=ps[:])
+            else:
+                nc.scalar.copy(out=tT[h][:], in_=ps[:])
+
+        PROD_BANK = (5, 6, 7, 3, 4, 5, 6, 7)
+        delta = {}
+
+        def product(a):
+            ps = bank(PROD_BANK[a], F32, "prod%d" % a)
+            nc.tensor.matmul(out=ps[:], lhsT=tT[a // 4][:, P * (a % 4) : P * (a % 4 + 1)], rhs=bT[a][:], start=True, stop=True)
+            delta[a] = sb([P, OUT], F32, "delta%d" % a)
+            nc.scalar.activation(
+                out=delta[a][:].rearrange("t (p j) -> t p j", j=4),
+                in_=ps[:].rearrange("t (j p) -> t p j", j=4),
+                func=COPY,
+                scale=2.0,
+            )
+
+        transpose_b(0)
+        transpose_t(0)
+        transpose_t(1)
+        transpose_b(1)
+        transpose_b(2)
+        for a in range(BLOCKS):
+            product(a)
+            if a + 3 < BLOCKS:
+                transpose_b(a + 3)
+
+        for r in range(EARLY_RUNS, len(SCALE_RUNS)):
+            load_run(r)
+
+        acc = {}
+
+        def mm(b, g):
+            if g == 0:
+                acc[b] = bank(b, F32, "acc%d" % b)
+            nc.tensor.matmul_mx(
+                out=acc[b][:],
+                lhsT=d_code[g][:, 2 * P * b : 2 * P * (b + 1)].bitcast(FP4),
+                lhsT_scale=d_plane[g][:, P * b : P * (b + 1)],
+                rhs=w_code[g].bitcast(FP4),
+                rhs_scale=w_plane[g],
+                start=(g == 0),
+                stop=(g == PASSES - 1),
+            )
+
+        for g in range(G1):
+            for b in range(BLOCKS):
+                mm(b, g)
+        for b in range(BLOCKS):
+            for g in range(G1, PASSES):
+                mm(b, g)
+            res = sb([P, OUT], F32, "res%d" % b)
+            if b < BLOCKS - 1:
+                nc.vector.tensor_tensor(out=res[:], in0=acc[b][:], in1=delta[b][:], op=ADD)
+                nc.sync.dma_start(out=out[b], in_=res[:])
+            else:
+                for h, eng in ((0, nc.sync), (1, nc.scalar)):
+                    cols = slice(256 * h, 256 * (h + 1))
+                    nc.vector.tensor_tensor(out=res[:, cols], in0=acc[b][:, cols], in1=delta[b][:, cols], op=ADD)
+                    eng.dma_start(out=out[b][:, cols], in_=res[:, cols])

@@ -20,7 +20,7 @@ TOKENS = 1024
 FLOPS = 2 * TOKENS * OUT * 8192 + 2 * TOKENS * OUT * RANK
 
 N_WARM = 5
-G1 = 10
+G1 = 13
 SCALE_RUNS = ((0, 2), (2, 6), (6, 10), (10, 16))
 B_CHUNKS = ((0, 1), (1, 4), (4, 8))
 EARLY_RUNS = 2
@@ -54,34 +54,38 @@ def tile_linear_pa_kernel(tc, data_words, data_scales, W_words, W_scales, t_lora
             for a in range(a0, a1):
                 b_raw[a] = raw[:, a - a0, :]
 
-        load_b(0)
-        nc.sync.dma_start(out=t_raw[:], in_=t_lora.rearrange("a g s r -> s (a g) r"))
-        load_b(1)
-        load_b(2)
-
         d_plane = {}
         w_plane = {}
         d_code = {}
         w_code = {}
+        planes = {}
 
-        def load_run(r):
+        def zero_planes(r):
             g0, g1 = SCALE_RUNS[r]
             dpl = sb([P, g1 - g0, TOKENS], U8, "dpl%d" % r)
             wpl = sb([P, g1 - g0, OUT], U8, "wpl%d" % r)
-            nc.vector.memset(dpl[:].bitcast(I32), 0)
             nc.vector.memset(wpl[:].bitcast(I32), 0)
-            for q in range(4):
-                nc.sync.dma_start(
-                    out=wpl[32 * q : 32 * q + 4, :, :].bitcast(I32),
-                    in_=W_scales[g0:g1, 4 * q : 4 * q + 4, :].rearrange("g r n -> r g n").bitcast(I32),
-                )
-                nc.sync.dma_start(
-                    out=dpl[32 * q : 32 * q + 4, :, :].bitcast(I32),
-                    in_=data_scales[g0:g1, 4 * q : 4 * q + 4, :].rearrange("g r n -> r g n").bitcast(I32),
-                )
+            nc.vector.memset(dpl[:].bitcast(I32), 0)
+            planes[r] = (wpl, dpl)
             for g in range(g0, g1):
                 d_plane[g] = dpl[:, g - g0, :]
                 w_plane[g] = wpl[:, g - g0, :]
+
+        def load_scales(r, rows):
+            g0, g1 = SCALE_RUNS[r]
+            wpl, dpl = planes[r]
+            for k in rows:
+                nc.sync.dma_start(
+                    out=wpl[k : P : 32, :, :].bitcast(I32),
+                    in_=W_scales[g0:g1, k : 16 : 4, :].rearrange("g q n -> q g n").bitcast(I32),
+                )
+                nc.sync.dma_start(
+                    out=dpl[k : P : 32, :, :].bitcast(I32),
+                    in_=data_scales[g0:g1, k : 16 : 4, :].rearrange("g q n -> q g n").bitcast(I32),
+                )
+
+        def load_codes(r):
+            g0, g1 = SCALE_RUNS[r]
             for g in range(g0, g1, 2):
                 wc = sb([P, 2, 2 * OUT], U8, "wc%d" % g)
                 nc.sync.dma_start(
@@ -94,8 +98,17 @@ def tile_linear_pa_kernel(tc, data_words, data_scales, W_words, W_scales, t_lora
                     nc.sync.dma_start(out=dc[:].bitcast(I32), in_=data_words[h].bitcast(I32))
                     d_code[h] = dc
 
-        for r in range(EARLY_RUNS):
-            load_run(r)
+        load_b(0)
+        nc.sync.dma_start(out=t_raw[:], in_=t_lora.rearrange("a g s r -> s (a g) r"))
+        load_b(1)
+        zero_planes(0)
+        load_scales(0, (0, 1))
+        load_b(2)
+        load_scales(0, (2, 3))
+        load_codes(0)
+        zero_planes(1)
+        load_scales(1, (0, 1, 2, 3))
+        load_codes(1)
 
         scr = sb([P, 1], F32, "scr")
         nc.scalar.activation(out=scr[:], in_=warm[:, 0:1], func=COPY, scale=2.0)
@@ -104,58 +117,57 @@ def tile_linear_pa_kernel(tc, data_words, data_scales, W_words, W_scales, t_lora
             nc.tensor.matmul(out=wps[:], lhsT=warm[:, 0:P], rhs=warm[:], start=True, stop=True)
 
         bT = {}
-
-        def transpose_b(a):
-            ps = bank(a % 3, BF16, "bTp%d" % a)
-            for j in range(4):
-                nc.tensor.transpose(out=ps[:, P * j : P * (j + 1)], in_=b_raw[a][:, P * j : P * (j + 1)], identity=ident[:])
-            bT[a] = sb([P, 512], BF16, "bT%d" % a)
-            nc.vector.tensor_copy(out=bT[a][:], in_=ps[:])
-
-        tT = []
-
-        def transpose_t(h):
-            ps = bank(3 + h, BF16, "tTp%d" % h)
-            for j in range(4):
-                nc.tensor.transpose(out=ps[:, P * j : P * (j + 1)], in_=t_raw[:, 4 * h + j, :], identity=ident[:])
-            tT.append(sb([P, 512], BF16, "tT%d" % h))
-            if h == 0:
-                nc.vector.tensor_copy(out=tT[h][:], in_=ps[:])
-            else:
-                nc.scalar.copy(out=tT[h][:], in_=ps[:])
-
-        PROD_BANK = (5, 6, 7, 3, 4, 5, 6, 7)
+        tT = {}
         delta = {}
 
-        def product(a):
-            ps = bank(PROD_BANK[a], F32, "prod%d" % a)
+        def copy_bf16(eng, dst, src):
+            if eng == 0:
+                nc.vector.tensor_copy(out=dst, in_=src)
+            else:
+                nc.scalar.copy(out=dst, in_=src)
+
+        def transpose_group(kind, i, bk, eng):
+            ps = bank(bk, BF16, "%sTp%d" % (kind, i))
+            for j in range(4):
+                src = b_raw[i][:, P * j : P * (j + 1)] if kind == "b" else t_raw[:, 4 * i + j, :]
+                nc.tensor.transpose(out=ps[:, P * j : P * (j + 1)], in_=src, identity=ident[:])
+            dst = sb([P, 512], BF16, "%sT%d" % (kind, i))
+            copy_bf16(eng, dst[:], ps[:])
+            if kind == "b":
+                bT[i] = dst
+            else:
+                tT[i] = dst
+
+        def product(a, bk, eng):
+            ps = bank(bk, F32, "prod%d" % a)
             nc.tensor.matmul(out=ps[:], lhsT=tT[a // 4][:, P * (a % 4) : P * (a % 4 + 1)], rhs=bT[a][:], start=True, stop=True)
             delta[a] = sb([P, OUT], F32, "delta%d" % a)
-            nc.scalar.activation(
-                out=delta[a][:].rearrange("t (p j) -> t p j", j=4),
-                in_=ps[:].rearrange("t (j p) -> t p j", j=4),
-                func=COPY,
-                scale=2.0,
-            )
+            dst = delta[a][:].rearrange("t (p j) -> t p j", j=4)
+            src = ps[:].rearrange("t (j p) -> t p j", j=4)
+            if eng == 0:
+                nc.vector.tensor_scalar_mul(out=dst, in0=src, scalar1=2.0)
+            else:
+                nc.scalar.activation(out=dst, in_=src, func=COPY, scale=2.0)
 
-        transpose_b(0)
-        transpose_t(0)
-        transpose_t(1)
-        transpose_b(1)
-        transpose_b(2)
-        for a in range(BLOCKS):
-            product(a)
-            if a + 3 < BLOCKS:
-                transpose_b(a + 3)
+        for n, (kind, i) in enumerate((("b", 0), ("t", 0), ("t", 1), ("b", 1), ("b", 2), ("b", 3))):
+            transpose_group(kind, i, n, n % 2)
+        for a in range(4):
+            product(a, (6 + a) % 8, a % 2)
+        for a in range(4, 8):
+            transpose_group("b", a, a - 2, a % 2)
+        for a in range(4, 8):
+            product(a, (2 + a) % 8, a % 2)
 
         for r in range(EARLY_RUNS, len(SCALE_RUNS)):
-            load_run(r)
+            zero_planes(r)
+            load_scales(r, (0, 1, 2, 3))
+            load_codes(r)
 
         acc = {}
 
         def mm(b, g):
             if g == 0:
-                acc[b] = bank(b, F32, "acc%d" % b)
+                acc[b] = bank((b + 2) % 8, F32, "acc%d" % b)
             nc.tensor.matmul_mx(
                 out=acc[b][:],
                 lhsT=d_code[g][:, 2 * P * b : 2 * P * (b + 1)].bitcast(FP4),

@@ -21,9 +21,11 @@ FLOPS = 2 * TOKENS * OUT * 8192 + 2 * TOKENS * OUT * RANK
 
 N_WARM = 5
 G1 = 13
-SCALE_RUNS = ((0, 2), (2, 6), (6, 10), (10, 16))
-B_CHUNKS = ((0, 1), (1, 4), (4, 8))
-EARLY_RUNS = 2
+SCALE_RUNS = ((0, 3), (3, 7), (7, 11), (11, 16))
+B_CHUNKS = ((0, 1), (1, 4), (4, 6), (6, 8))
+HEAD_PASSES = 7
+UNITS = tuple((b, 0, 512, (3, 2, 0, 1, 4, 5, 6)[b]) for b in range(7)) + ((7, 0, 256, 7), (7, 256, 256, 3))
+SCALAR_PRODUCTS = (0, 2, 3, 5, 6)
 
 
 def tile_linear_pa_kernel(tc, data_words, data_scales, W_words, W_scales, t_lora, lora_b, out):
@@ -33,8 +35,8 @@ def tile_linear_pa_kernel(tc, data_words, data_scales, W_words, W_scales, t_lora
         psum = ctx.enter_context(tc.psum_pool(name="psum", bufs=1))
         ctx.enter_context(tc.manual_schedule())
 
-        def bank(i, dtype, name):
-            return psum.tile([P, 512], dtype, tag="bank%d" % i, name=name)
+        def bank(i, shape, dtype, name):
+            return psum.tile(shape, dtype, tag="bank%d" % i, name=name)
 
         def sb(shape, dtype, name):
             return keep.tile(shape, dtype, tag=name, name=name, align_bytes=64)
@@ -45,7 +47,7 @@ def tile_linear_pa_kernel(tc, data_words, data_scales, W_words, W_scales, t_lora
         make_identity(nc, ident[:])
 
         b_raw = {}
-        t_raw = sb([P, BLOCKS, RANK], BF16, "t_raw")
+        t_raw = sb([P, 8, RANK], BF16, "t_raw")
 
         def load_b(c):
             a0, a1 = B_CHUNKS[c]
@@ -84,35 +86,41 @@ def tile_linear_pa_kernel(tc, data_words, data_scales, W_words, W_scales, t_lora
                     in_=data_scales[g0:g1, k : 16 : 4, :].rearrange("g q n -> q g n").bitcast(I32),
                 )
 
-        def load_codes(r):
-            g0, g1 = SCALE_RUNS[r]
-            for g in range(g0, g1, 2):
-                wc = sb([P, 2, 2 * OUT], U8, "wc%d" % g)
-                nc.sync.dma_start(
-                    out=wc[:].bitcast(I32),
-                    in_=W_words[g : g + 2].rearrange("g p n -> p g n").bitcast(I32),
-                )
-                for h in (g, g + 1):
-                    w_code[h] = wc[:, h - g, :]
-                    dc = sb([P, 2 * TOKENS], U8, "dc%d" % h)
-                    nc.sync.dma_start(out=dc[:].bitcast(I32), in_=data_words[h].bitcast(I32))
-                    d_code[h] = dc
+        def load_w(g):
+            wc = sb([P, 2, 2 * OUT], U8, "wc%d" % g)
+            nc.sync.dma_start(out=wc[:].bitcast(I32), in_=W_words[g : g + 2].rearrange("g p n -> p g n").bitcast(I32))
+            w_code[g] = wc[:, 0, :]
+            w_code[g + 1] = wc[:, 1, :]
+
+        def load_d(g):
+            d_code[g] = sb([P, 2 * TOKENS], U8, "dc%d" % g)
+            nc.sync.dma_start(out=d_code[g][:].bitcast(I32), in_=data_words[g].bitcast(I32))
+
+        def load_passes(g0, g1):
+            for g in range(g0, g1):
+                if g % 2 == 0:
+                    load_w(g)
+                for r in range(1, len(SCALE_RUNS)):
+                    if SCALE_RUNS[r][0] == g:
+                        zero_planes(r)
+                        load_scales(r, (0, 1, 2, 3))
+                load_d(g)
 
         load_b(0)
-        nc.sync.dma_start(out=t_raw[:], in_=t_lora.rearrange("a g s r -> s (a g) r"))
+        nc.sync.dma_start(out=t_raw[:], in_=t_lora.rearrange("a g s r -> (a g s) r").rearrange("(p j) r -> p j r", j=8))
         load_b(1)
         zero_planes(0)
         load_scales(0, (0, 1))
         load_b(2)
+        load_b(3)
+        load_w(0)
+        load_d(0)
         load_scales(0, (2, 3))
-        load_codes(0)
-        zero_planes(1)
-        load_scales(1, (0, 1, 2, 3))
-        load_codes(1)
+        load_passes(1, HEAD_PASSES)
 
         scr = sb([P, 1], F32, "scr")
         nc.scalar.activation(out=scr[:], in_=warm[:, 0:1], func=COPY, scale=2.0)
-        wps = bank(7, F32, "wps")
+        wps = bank(7, [P, 512], F32, "wps")
         for i in range(N_WARM):
             nc.tensor.matmul(out=wps[:], lhsT=warm[:, 0:P], rhs=warm[:], start=True, stop=True)
 
@@ -120,76 +128,78 @@ def tile_linear_pa_kernel(tc, data_words, data_scales, W_words, W_scales, t_lora
         tT = {}
         delta = {}
 
-        def copy_bf16(eng, dst, src):
-            if eng == 0:
-                nc.vector.tensor_copy(out=dst, in_=src)
-            else:
-                nc.scalar.copy(out=dst, in_=src)
+        def turn(dst, src):
+            nc.tensor.transpose(out=dst, in_=src, identity=ident[:])
 
-        def transpose_group(kind, i, bk, eng):
-            ps = bank(bk, BF16, "%sTp%d" % (kind, i))
+        def turn_b(a):
+            ps = bank(a % 3, [P, 512], BF16, "bTp%d" % a)
             for j in range(4):
-                src = b_raw[i][:, P * j : P * (j + 1)] if kind == "b" else t_raw[:, 4 * i + j, :]
-                nc.tensor.transpose(out=ps[:, P * j : P * (j + 1)], in_=src, identity=ident[:])
-            dst = sb([P, 512], BF16, "%sT%d" % (kind, i))
-            copy_bf16(eng, dst[:], ps[:])
-            if kind == "b":
-                bT[i] = dst
-            else:
-                tT[i] = dst
+                turn(ps[:, P * j : P * (j + 1)], b_raw[a][:, P * j : P * (j + 1)])
+            bT[a] = sb([P, 512], BF16, "bT%d" % a)
+            nc.vector.tensor_copy(out=bT[a][:], in_=ps[:])
 
-        def product(a, bk, eng):
-            ps = bank(bk, F32, "prod%d" % a)
+        def turn_t():
+            ps = bank(3, [P, TOKENS], BF16, "tTp")
+            for j in range(8):
+                turn(ps[:, P * j : P * (j + 1)], t_raw[:, j, :])
+            for h in range(2):
+                tT[h] = sb([P, 512], BF16, "tT%d" % h)
+                nc.scalar.copy(
+                    out=tT[h][:].rearrange("r (p j) -> r p j", j=8),
+                    in_=ps[:].rearrange("r (j p) -> r p j", j=8)[:, 64 * h : 64 * (h + 1), :],
+                )
+
+        def product(a):
+            ps = bank(4 + a % 4, [P, 512], F32, "prod%d" % a)
             nc.tensor.matmul(out=ps[:], lhsT=tT[a // 4][:, P * (a % 4) : P * (a % 4 + 1)], rhs=bT[a][:], start=True, stop=True)
             delta[a] = sb([P, OUT], F32, "delta%d" % a)
             dst = delta[a][:].rearrange("t (p j) -> t p j", j=4)
             src = ps[:].rearrange("t (j p) -> t p j", j=4)
-            if eng == 0:
-                nc.vector.tensor_scalar_mul(out=dst, in0=src, scalar1=2.0)
-            else:
+            if a in SCALAR_PRODUCTS:
                 nc.scalar.activation(out=dst, in_=src, func=COPY, scale=2.0)
+            else:
+                nc.vector.tensor_scalar_mul(out=dst, in0=src, scalar1=2.0)
 
-        for n, (kind, i) in enumerate((("b", 0), ("t", 0), ("t", 1), ("b", 1), ("b", 2), ("b", 3))):
-            transpose_group(kind, i, n, n % 2)
-        for a in range(4):
-            product(a, (6 + a) % 8, a % 2)
-        for a in range(4, 8):
-            transpose_group("b", a, a - 2, a % 2)
-        for a in range(4, 8):
-            product(a, (2 + a) % 8, a % 2)
+        turn_b(0)
+        turn_t()
+        turn_b(1)
+        turn_b(2)
+        for a in range(BLOCKS):
+            product(a)
+            if a + 3 < BLOCKS:
+                turn_b(a + 3)
 
-        for r in range(EARLY_RUNS, len(SCALE_RUNS)):
-            zero_planes(r)
-            load_scales(r, (0, 1, 2, 3))
-            load_codes(r)
+        load_passes(HEAD_PASSES, PASSES)
 
         acc = {}
 
-        def mm(b, g):
+        def mm(u, g):
+            b, c0, n, bk = UNITS[u]
             if g == 0:
-                acc[b] = bank((b + 2) % 8, F32, "acc%d" % b)
+                acc[u] = bank(bk, [P, 512], F32, "acc%d" % u)
             nc.tensor.matmul_mx(
-                out=acc[b][:],
+                out=acc[u][:, 0:n],
                 lhsT=d_code[g][:, 2 * P * b : 2 * P * (b + 1)].bitcast(FP4),
                 lhsT_scale=d_plane[g][:, P * b : P * (b + 1)],
-                rhs=w_code[g].bitcast(FP4),
-                rhs_scale=w_plane[g],
+                rhs=w_code[g][:, 2 * c0 : 2 * (c0 + n)].bitcast(FP4),
+                rhs_scale=w_plane[g][:, c0 : c0 + n],
                 start=(g == 0),
                 stop=(g == PASSES - 1),
             )
 
+        def finish(u):
+            b, c0, n, bk = UNITS[u]
+            res = sb([P, n], F32, "res%d" % u)
+            nc.vector.tensor_tensor(out=res[:], in0=acc[u][:, 0:n], in1=delta[b][:, c0 : c0 + n], op=ADD)
+            nc.sync.dma_start(out=out[b][:, c0 : c0 + n], in_=res[:])
+
         for g in range(G1):
-            for b in range(BLOCKS):
-                mm(b, g)
-        for b in range(BLOCKS):
+            for u in range(8):
+                mm(u, g)
+        for u in range(8):
             for g in range(G1, PASSES):
-                mm(b, g)
-            res = sb([P, OUT], F32, "res%d" % b)
-            if b < BLOCKS - 1:
-                nc.vector.tensor_tensor(out=res[:], in0=acc[b][:], in1=delta[b][:], op=ADD)
-                nc.sync.dma_start(out=out[b], in_=res[:])
-            else:
-                for h, eng in ((0, nc.sync), (1, nc.scalar)):
-                    cols = slice(256 * h, 256 * (h + 1))
-                    nc.vector.tensor_tensor(out=res[:, cols], in0=acc[b][:, cols], in1=delta[b][:, cols], op=ADD)
-                    eng.dma_start(out=out[b][:, cols], in_=res[:, cols])
+                mm(u, g)
+            finish(u)
+        for g in range(PASSES):
+            mm(8, g)
+        finish(8)

@@ -19,13 +19,13 @@ RANK = 128
 TOKENS = 1024
 FLOPS = 2 * TOKENS * OUT * 8192 + 2 * TOKENS * OUT * RANK
 
-N_WARM = 5
+N_WARM = 4
 G1 = 13
 SCALE_RUNS = ((0, 3), (3, 7), (7, 11), (11, 16))
 B_CHUNKS = ((0, 1), (1, 4), (4, 6), (6, 8))
 HEAD_PASSES = 7
 UNITS = tuple((b, 0, 512, (3, 2, 0, 1, 4, 5, 6)[b]) for b in range(7)) + ((7, 0, 256, 7), (7, 256, 256, 3))
-SCALAR_PRODUCTS = (0, 2, 3, 5, 6)
+SCALAR_PRODUCTS = (0, 1, 2, 3, 4, 5, 6, 7)
 
 
 def tile_linear_pa_kernel(tc, data_words, data_scales, W_words, W_scales, t_lora, lora_b, out):
@@ -121,8 +121,11 @@ def tile_linear_pa_kernel(tc, data_words, data_scales, W_words, W_scales, t_lora
         scr = sb([P, 1], F32, "scr")
         nc.scalar.activation(out=scr[:], in_=warm[:, 0:1], func=COPY, scale=2.0)
         wps = bank(7, [P, 512], F32, "wps")
-        for i in range(N_WARM):
-            nc.tensor.matmul(out=wps[:], lhsT=warm[:, 0:P], rhs=warm[:], start=True, stop=True)
+        def idle_matmuls(n):
+            for i in range(n):
+                nc.tensor.matmul(out=wps[:], lhsT=warm[:, 0:P], rhs=warm[:], start=True, stop=True)
+
+        idle_matmuls(N_WARM)
 
         bT = {}
         tT = {}
@@ -161,7 +164,9 @@ def tile_linear_pa_kernel(tc, data_words, data_scales, W_words, W_scales, t_lora
                 nc.vector.tensor_scalar_mul(out=dst, in0=src, scalar1=2.0)
 
         turn_b(0)
+        idle_matmuls(1)
         turn_t()
+        idle_matmuls(1)
         turn_b(1)
         turn_b(2)
         for a in range(BLOCKS):

@@ -22,7 +22,7 @@ FLOPS = 2 * TOKENS * OUT * 8192 + 2 * TOKENS * OUT * RANK
 N_WARM = 4
 G1 = 13
 SCALE_RUNS = ((0, 3), (3, 7), (7, 11), (11, 16))
-B_CHUNKS = ((0, 1), (1, 4), (4, 6), (6, 8))
+B_CHUNKS = ((0, 1), (1, 3), (3, 6), (6, 8))
 HEAD_PASSES = 7
 UNITS = tuple((b, 0, 512, (3, 2, 0, 1, 4, 5, 6)[b]) for b in range(7)) + ((7, 0, 256, 7), (7, 256, 256, 3))
 SCALAR_PRODUCTS = (0, 1, 2, 3, 4, 5, 6, 7)
@@ -147,7 +147,8 @@ def tile_linear_pa_kernel(tc, data_words, data_scales, W_words, W_scales, t_lora
                 turn(ps[:, P * j : P * (j + 1)], t_raw[:, j, :])
             for h in range(2):
                 tT[h] = sb([P, 512], BF16, "tT%d" % h)
-                nc.scalar.copy(
+                copy = nc.vector.tensor_copy if h == 0 else nc.scalar.copy
+                copy(
                     out=tT[h][:].rearrange("r (p j) -> r p j", j=8),
                     in_=ps[:].rearrange("r (j p) -> r p j", j=8)[:, 64 * h : 64 * (h + 1), :],
                 )
@@ -166,7 +167,6 @@ def tile_linear_pa_kernel(tc, data_words, data_scales, W_words, W_scales, t_lora
         turn_b(0)
         idle_matmuls(1)
         turn_t()
-        idle_matmuls(1)
         turn_b(1)
         turn_b(2)
         for a in range(BLOCKS):

@@ -21,9 +21,9 @@ FLOPS = 2 * TOKENS * OUT * 8192 + 2 * TOKENS * OUT * RANK
 
 N_WARM = 4
 G1 = 13
-SCALE_RUNS = ((0, 3), (3, 7), (7, 11), (11, 16))
+SCALE_RUNS = ((0, 2), (2, 6), (6, 11), (11, 16))
 B_CHUNKS = ((0, 1), (1, 3), (3, 6), (6, 8))
-HEAD_PASSES = 7
+HEAD_PASSES = 6
 UNITS = tuple((b, 0, 512, (3, 2, 0, 1, 4, 5, 6)[b]) for b in range(7)) + ((7, 0, 256, 7), (7, 256, 256, 3))
 SCALAR_PRODUCTS = (0, 1, 2, 3, 4, 5, 6, 7)
 
@@ -92,6 +92,11 @@ def tile_linear_pa_kernel(tc, data_words, data_scales, W_words, W_scales, t_lora
             w_code[g] = wc[:, 0, :]
             w_code[g + 1] = wc[:, 1, :]
 
+        def load_w_single(g):
+            wc = sb([P, 2 * OUT], U8, "wc%d" % g)
+            nc.sync.dma_start(out=wc[:].bitcast(I32), in_=W_words[g].bitcast(I32))
+            w_code[g] = wc[:]
+
         def load_d(g):
             d_code[g] = sb([P, 2 * TOKENS], U8, "dc%d" % g)
             nc.sync.dma_start(out=d_code[g][:].bitcast(I32), in_=data_words[g].bitcast(I32))
@@ -113,9 +118,10 @@ def tile_linear_pa_kernel(tc, data_words, data_scales, W_words, W_scales, t_lora
         load_scales(0, (0, 1))
         load_b(2)
         load_b(3)
-        load_w(0)
-        load_d(0)
         load_scales(0, (2, 3))
+        load_w_single(0)
+        load_d(0)
+        load_w_single(1)
         load_passes(1, HEAD_PASSES)
 
         scr = sb([P, 1], F32, "scr")

@@ -25,7 +25,7 @@ SCALE_RUNS = ((0, 2), (2, 6), (6, 11), (11, 16))
 B_CHUNKS = ((0, 1), (1, 3), (3, 6), (6, 8))
 HEAD_PASSES = 6
 UNITS = tuple((b, 0, 512, (3, 2, 0, 1, 4, 5, 6)[b]) for b in range(7)) + ((7, 0, 256, 7), (7, 256, 256, 3))
-SCALAR_PRODUCTS = (0, 1, 2, 3, 4, 5, 6, 7)
+SCALAR_PRODUCTS = (0, 1, 2, 3, 4, 6)
 
 
 def tile_linear_pa_kernel(tc, data_words, data_scales, W_words, W_scales, t_lora, lora_b, out):

@@ -19,7 +19,7 @@ RANK = 128
 TOKENS = 1024
 FLOPS = 2 * TOKENS * OUT * 8192 + 2 * TOKENS * OUT * RANK
 
-N_WARM = 4
+N_WARM = 16
 G1 = 13
 SCALE_RUNS = ((0, 2), (2, 6), (6, 11), (11, 16))
 B_CHUNKS = ((0, 1), (1, 3), (3, 6), (6, 8))
@@ -41,6 +41,8 @@ def tile_linear_pa_kernel(tc, data_words, data_scales, W_words, W_scales, t_lora
         def sb(shape, dtype, name):
             return keep.tile(shape, dtype, tag=name, name=name, align_bytes=64)
 
+        first = sb([P, P], BF16, "first")
+        nc.gpsimd.memset(first[:], 0.0)
         warm = sb([P, 512], BF16, "warm")
         nc.vector.memset(warm[:], 0.0)
         ident = sb([P, P], BF16, "ident")
@@ -131,7 +133,8 @@ def tile_linear_pa_kernel(tc, data_words, data_scales, W_words, W_scales, t_lora
             for i in range(n):
                 nc.tensor.matmul(out=wps[:], lhsT=warm[:, 0:P], rhs=warm[:], start=True, stop=True)
 
-        idle_matmuls(N_WARM)
+        for i in range(N_WARM):
+            nc.tensor.matmul(out=wps[:, 0:P], lhsT=first[:], rhs=first[:], start=True, stop=True)
 
         bT = {}
         tT = {}

@@ -24,7 +24,9 @@ G1 = 13
 SCALE_RUNS = ((0, 2), (2, 6), (6, 11), (11, 16))
 B_CHUNKS = ((0, 1), (1, 3), (3, 6), (6, 8))
 HEAD_PASSES = 6
-UNITS = tuple((b, 0, 512, (3, 2, 0, 1, 4, 5, 6)[b]) for b in range(7)) + ((7, 0, 256, 7), (7, 256, 256, 3))
+MX_BANK = (2, 0, 1, 7, 3, 4, 5, 6)
+PRODUCT_BANK = (4, 5, 6, 7, 3, 4, 5, 6)
+UNITS = tuple((b, 0, 512, MX_BANK[b]) for b in range(7)) + ((7, 0, 256, MX_BANK[7]), (7, 256, 256, MX_BANK[0]))
 SCALAR_PRODUCTS = (0, 1, 2, 3, 4, 6)
 
 
@@ -163,7 +165,7 @@ def tile_linear_pa_kernel(tc, data_words, data_scales, W_words, W_scales, t_lora
                 )
 
         def product(a):
-            ps = bank(4 + a % 4, [P, 512], F32, "prod%d" % a)
+            ps = bank(PRODUCT_BANK[a], [P, 512], F32, "prod%d" % a)
             nc.tensor.matmul(out=ps[:], lhsT=tT[a // 4][:, P * (a % 4) : P * (a % 4 + 1)], rhs=bT[a][:], start=True, stop=True)
             delta[a] = sb([P, OUT], F32, "delta%d" % a)
             dst = delta[a][:].rearrange("t (p j) -> t p j", j=4)

@@ -41,7 +41,7 @@ def tile_linear_pa_kernel(tc, data_words, data_scales, W_words, W_scales, t_lora
             return psum.tile(shape, dtype, tag="bank%d" % i, name=name)
 
         def sb(shape, dtype, name):
-            return keep.tile(shape, dtype, tag=name, name=name, align_bytes=64)
+            return keep.tile(shape, dtype, tag=name, name=name, align_bytes=256)
 
         first = sb([P, P], BF16, "first")
         nc.gpsimd.memset(first[:], 0.0)

@@ -22,10 +22,11 @@ FLOPS = 2 * TOKENS * OUT * 8192 + 2 * TOKENS * OUT * RANK
 N_WARM = 16
 G1 = 13
 SCALE_RUNS = ((0, 2), (2, 6), (6, 11), (11, 16))
-B_CHUNKS = ((0, 1), (1, 3), (3, 6), (6, 8))
+B_CHUNKS = ((0, 1), (1, 2), (2, 4), (4, 6), (6, 8))
 HEAD_PASSES = 6
-MX_BANK = (2, 0, 1, 7, 3, 4, 5, 6)
-PRODUCT_BANK = (4, 5, 6, 7, 3, 4, 5, 6)
+MX_BANK = (2, 0, 1, 3, 4, 5, 6, 7)
+PRODUCT_BANK = (5, 6, 7, 3, 4, 5, 6, 7)
+T_BANK = (3, 4)
 UNITS = tuple((b, 0, 512, MX_BANK[b]) for b in range(7)) + ((7, 0, 256, MX_BANK[7]), (7, 256, 256, MX_BANK[0]))
 SCALAR_PRODUCTS = (0, 1, 2, 3, 4, 6)
 
@@ -43,22 +44,26 @@ def tile_linear_pa_kernel(tc, data_words, data_scales, W_words, W_scales, t_lora
         def sb(shape, dtype, name):
             return keep.tile(shape, dtype, tag=name, name=name, align_bytes=256)
 
-        first = sb([P, P], BF16, "first")
-        nc.gpsimd.memset(first[:], 0.0)
-        warm = sb([P, 512], BF16, "warm")
-        nc.vector.memset(warm[:], 0.0)
-        ident = sb([P, P], BF16, "ident")
-        make_identity(nc, ident[:])
-
         b_raw = {}
-        t_raw = sb([P, 8, RANK], BF16, "t_raw")
+        t_raw = {}
 
-        def load_b(c):
+        def load_b(c, queue):
             a0, a1 = B_CHUNKS[c]
             raw = sb([P, a1 - a0, 4 * RANK], BF16, "b_raw%d" % c)
-            nc.sync.dma_start(out=raw[:], in_=lora_b[a0:a1].rearrange("a (p j) r -> p a (j r)", j=4))
+            queue.dma_start(out=raw[:], in_=lora_b[a0:a1].rearrange("a (p j) r -> p a (j r)", j=4))
             for a in range(a0, a1):
                 b_raw[a] = raw[:, a - a0, :]
+
+        def load_t():
+            raw = sb([P, 2, 4 * RANK], BF16, "t_raw")
+            nc.sync.dma_start(out=raw[:], in_=t_lora.rearrange("a g s r -> (a g s) r").rearrange("(h p j) r -> p h (j r)", h=2, j=4))
+            for h in range(2):
+                t_raw[h] = raw[:, h, :]
+
+        first = sb([P, P], BF16, "first")
+        nc.gpsimd.memset(first[:], 0.0)
+        ident = sb([P, P], BF16, "ident")
+        make_identity(nc, ident[:])
 
         d_plane = {}
         w_plane = {}
@@ -77,18 +82,17 @@ def tile_linear_pa_kernel(tc, data_words, data_scales, W_words, W_scales, t_lora
                 d_plane[g] = dpl[:, g - g0, :]
                 w_plane[g] = wpl[:, g - g0, :]
 
-        def load_scales(r, rows):
+        def load_scale(r, i):
             g0, g1 = SCALE_RUNS[r]
-            wpl, dpl = planes[r]
-            for k in rows:
-                nc.sync.dma_start(
-                    out=wpl[k : P : 32, :, :].bitcast(I32),
-                    in_=W_scales[g0:g1, k : 16 : 4, :].rearrange("g q n -> q g n").bitcast(I32),
-                )
-                nc.sync.dma_start(
-                    out=dpl[k : P : 32, :, :].bitcast(I32),
-                    in_=data_scales[g0:g1, k : 16 : 4, :].rearrange("g q n -> q g n").bitcast(I32),
-                )
+            k = i // 2
+            nc.sync.dma_start(
+                out=planes[r][i % 2][k : P : 32, :, :].bitcast(I32),
+                in_=(W_scales, data_scales)[i % 2][g0:g1, k : 16 : 4, :].rearrange("g q n -> q g n").bitcast(I32),
+            )
+
+        def load_scales(r, first_i, end_i):
+            for i in range(first_i, end_i):
+                load_scale(r, i)
 
         def load_w(g):
             wc = sb([P, 2, 2 * OUT], U8, "wc%d" % g)
@@ -112,29 +116,26 @@ def tile_linear_pa_kernel(tc, data_words, data_scales, W_words, W_scales, t_lora
                 for r in range(1, len(SCALE_RUNS)):
                     if SCALE_RUNS[r][0] == g:
                         zero_planes(r)
-                        load_scales(r, (0, 1, 2, 3))
+                        load_scales(r, 0, 8)
                 load_d(g)
 
-        load_b(0)
-        nc.sync.dma_start(out=t_raw[:], in_=t_lora.rearrange("a g s r -> (a g s) r").rearrange("(p j) r -> p j r", j=8))
-        load_b(1)
+        load_b(0, nc.sync)
+        load_t()
+        load_b(1, nc.sync)
+        load_b(2, nc.sync)
         zero_planes(0)
-        load_scales(0, (0, 1))
-        load_b(2)
-        load_b(3)
-        load_scales(0, (2, 3))
+        load_scales(0, 0, 4)
+        load_b(3, nc.sync)
+        load_b(4, nc.sync)
+        load_scales(0, 4, 8)
         load_w_single(0)
         load_d(0)
         load_w_single(1)
         load_passes(1, HEAD_PASSES)
 
         scr = sb([P, 1], F32, "scr")
-        nc.scalar.activation(out=scr[:], in_=warm[:, 0:1], func=COPY, scale=2.0)
+        nc.scalar.activation(out=scr[:], in_=first[:, 0:1], func=COPY, scale=2.0)
         wps = bank(7, [P, 512], F32, "wps")
-        def idle_matmuls(n):
-            for i in range(n):
-                nc.tensor.matmul(out=wps[:], lhsT=warm[:, 0:P], rhs=warm[:], start=True, stop=True)
-
         for i in range(N_WARM):
             nc.tensor.matmul(out=wps[:, 0:P], lhsT=first[:], rhs=first[:], start=True, stop=True)
 
@@ -150,19 +151,19 @@ def tile_linear_pa_kernel(tc, data_words, data_scales, W_words, W_scales, t_lora
             for j in range(4):
                 turn(ps[:, P * j : P * (j + 1)], b_raw[a][:, P * j : P * (j + 1)])
             bT[a] = sb([P, 512], BF16, "bT%d" % a)
-            nc.vector.tensor_copy(out=bT[a][:], in_=ps[:])
+            copy = nc.scalar.copy if a == 0 else nc.vector.tensor_copy
+            copy(out=bT[a][:], in_=ps[:])
 
-        def turn_t():
-            ps = bank(3, [P, TOKENS], BF16, "tTp")
-            for j in range(8):
-                turn(ps[:, P * j : P * (j + 1)], t_raw[:, j, :])
-            for h in range(2):
-                tT[h] = sb([P, 512], BF16, "tT%d" % h)
-                copy = nc.vector.tensor_copy if h == 0 else nc.scalar.copy
-                copy(
-                    out=tT[h][:].rearrange("r (p j) -> r p j", j=8),
-                    in_=ps[:].rearrange("r (j p) -> r p j", j=8)[:, 64 * h : 64 * (h + 1), :],
-                )
+        def turn_t(h):
+            ps = bank(T_BANK[h], [P, 512], BF16, "tTp%d" % h)
+            for j in range(4):
+                turn(ps[:, P * j : P * (j + 1)], t_raw[h][:, P * j : P * (j + 1)])
+            tT[h] = sb([P, 512], BF16, "tT%d" % h)
+            copy = nc.vector.tensor_copy if h == 0 else nc.scalar.copy
+            copy(
+                out=tT[h][:].rearrange("r (p j) -> r p j", j=4),
+                in_=ps[:].rearrange("r (j p) -> r p j", j=4),
+            )
 
         def product(a):
             ps = bank(PRODUCT_BANK[a], [P, 512], F32, "prod%d" % a)
@@ -176,17 +177,25 @@ def tile_linear_pa_kernel(tc, data_words, data_scales, W_words, W_scales, t_lora
                 nc.vector.tensor_scalar_mul(out=dst, in0=src, scalar1=2.0)
 
         turn_b(0)
-        idle_matmuls(1)
-        turn_t()
+        turn_t(0)
         turn_b(1)
+        turn_t(1)
         turn_b(2)
-        for a in range(BLOCKS):
-            product(a)
-            if a + 3 < BLOCKS:
-                turn_b(a + 3)
+        product(0)
+        product(1)
+        turn_b(3)
+        product(2)
+        turn_b(4)
+        turn_b(5)
+        product(3)
+        turn_b(6)
+        product(4)
+        turn_b(7)
+        product(5)
+        product(6)
+        product(7)
 
         load_passes(HEAD_PASSES, PASSES)
-
         acc = {}
 
         def mm(u, g):

@@ -151,16 +151,14 @@ def tile_linear_pa_kernel(tc, data_words, data_scales, W_words, W_scales, t_lora
             for j in range(4):
                 turn(ps[:, P * j : P * (j + 1)], b_raw[a][:, P * j : P * (j + 1)])
             bT[a] = sb([P, 512], BF16, "bT%d" % a)
-            copy = nc.scalar.copy if a == 0 else nc.vector.tensor_copy
-            copy(out=bT[a][:], in_=ps[:])
+            nc.vector.tensor_copy(out=bT[a][:], in_=ps[:])
 
         def turn_t(h):
             ps = bank(T_BANK[h], [P, 512], BF16, "tTp%d" % h)
             for j in range(4):
                 turn(ps[:, P * j : P * (j + 1)], t_raw[h][:, P * j : P * (j + 1)])
             tT[h] = sb([P, 512], BF16, "tT%d" % h)
-            copy = nc.vector.tensor_copy if h == 0 else nc.scalar.copy
-            copy(
+            nc.scalar.copy(
                 out=tT[h][:].rearrange("r (p j) -> r p j", j=4),
                 in_=ps[:].rearrange("r (j p) -> r p j", j=4),
             )
@@ -181,19 +179,10 @@ def tile_linear_pa_kernel(tc, data_words, data_scales, W_words, W_scales, t_lora
         turn_b(1)
         turn_t(1)
         turn_b(2)
-        product(0)
-        product(1)
-        turn_b(3)
-        product(2)
-        turn_b(4)
-        turn_b(5)
-        product(3)
-        turn_b(6)
-        product(4)
-        turn_b(7)
-        product(5)
-        product(6)
-        product(7)
+        for a in range(BLOCKS):
+            product(a)
+            if a + 3 < BLOCKS:
+                turn_b(a + 3)
 
         load_passes(HEAD_PASSES, PASSES)
         acc = {}

@@ -179,10 +179,11 @@ def tile_linear_pa_kernel(tc, data_words, data_scales, W_words, W_scales, t_lora
         turn_b(1)
         turn_t(1)
         turn_b(2)
+        turn_b(3)
         for a in range(BLOCKS):
             product(a)
-            if a + 3 < BLOCKS:
-                turn_b(a + 3)
+            if a + 4 < BLOCKS:
+                turn_b(a + 4)
 
         load_passes(HEAD_PASSES, PASSES)
         acc = {}

@@ -28,7 +28,7 @@ MX_BANK = (2, 0, 1, 3, 4, 5, 6, 7)
 PRODUCT_BANK = (5, 6, 7, 3, 4, 5, 6, 7)
 T_BANK = (3, 4)
 UNITS = tuple((b, 0, 512, MX_BANK[b]) for b in range(7)) + ((7, 0, 256, MX_BANK[7]), (7, 256, 256, MX_BANK[0]))
-SCALAR_PRODUCTS = (0, 1, 2, 3, 4, 6)
+SCALAR_PRODUCTS = (0, 1, 2, 3, 5)
 
 
 def tile_linear_pa_kernel(tc, data_words, data_scales, W_words, W_scales, t_lora, lora_b, out):

from contextlib import ExitStack

import concourse.mybir as mybir
from concourse.masks import make_identity

F32 = mybir.dt.float32
BF16 = mybir.dt.bfloat16
U8 = mybir.dt.uint8
I32 = mybir.dt.int32
FP4 = mybir.dt.float4_e2m1fn_x4
COPY = mybir.ActivationFunctionType.Copy
ADD = mybir.AluOpType.add

P = 128
PASSES = 16
BLOCKS = 8
OUT = 512
RANK = 128
TOKENS = 1024
FLOPS = 2 * TOKENS * OUT * 8192 + 2 * TOKENS * OUT * RANK

N_WARM = 16
G1 = 13
SCALE_RUNS = ((0, 2), (2, 6), (6, 11), (11, 16))
B_CHUNKS = ((0, 1), (1, 2), (2, 4), (4, 6), (6, 8))
HEAD_PASSES = 6
MX_BANK = (2, 0, 1, 3, 4, 5, 6, 7)
PRODUCT_BANK = (5, 6, 7, 3, 4, 5, 6, 7)
T_BANK = (3, 4)
UNITS = tuple((b, 0, 512, MX_BANK[b]) for b in range(7)) + ((7, 0, 256, MX_BANK[7]), (7, 256, 256, MX_BANK[0]))
SCALAR_PRODUCTS = (0, 1, 2, 3, 5)


def tile_linear_pa_kernel(tc, data_words, data_scales, W_words, W_scales, t_lora, lora_b, out):
    nc = tc.nc
    with ExitStack() as ctx:
        keep = ctx.enter_context(tc.tile_pool(name="keep", bufs=1))
        psum = ctx.enter_context(tc.psum_pool(name="psum", bufs=1))
        ctx.enter_context(tc.manual_schedule())

        def bank(i, shape, dtype, name):
            return psum.tile(shape, dtype, tag="bank%d" % i, name=name)

        def sb(shape, dtype, name):
            return keep.tile(shape, dtype, tag=name, name=name, align_bytes=256)

        b_raw = {}
        t_raw = {}

        def load_b(c, queue):
            a0, a1 = B_CHUNKS[c]
            raw = sb([P, a1 - a0, 4 * RANK], BF16, "b_raw%d" % c)
            queue.dma_start(out=raw[:], in_=lora_b[a0:a1].rearrange("a (p j) r -> p a (j r)", j=4))
            for a in range(a0, a1):
                b_raw[a] = raw[:, a - a0, :]

        def load_t():
            raw = sb([P, 2, 4 * RANK], BF16, "t_raw")
            nc.sync.dma_start(out=raw[:], in_=t_lora.rearrange("a g s r -> (a g s) r").rearrange("(h p j) r -> p h (j r)", h=2, j=4))
            for h in range(2):
                t_raw[h] = raw[:, h, :]

        first = sb([P, P], BF16, "first")
        nc.gpsimd.memset(first[:], 0.0)
        ident = sb([P, P], BF16, "ident")
        make_identity(nc, ident[:])

        d_plane = {}
        w_plane = {}
        d_code = {}
        w_code = {}
        planes = {}

        def zero_planes(r):
            g0, g1 = SCALE_RUNS[r]
            dpl = sb([P, g1 - g0, TOKENS], U8, "dpl%d" % r)
            wpl = sb([P, g1 - g0, OUT], U8, "wpl%d" % r)
            nc.vector.memset(wpl[:].bitcast(I32), 0)
            nc.vector.memset(dpl[:].bitcast(I32), 0)
            planes[r] = (wpl, dpl)
            for g in range(g0, g1):
                d_plane[g] = dpl[:, g - g0, :]
                w_plane[g] = wpl[:, g - g0, :]

        def load_scale(r, i):
            g0, g1 = SCALE_RUNS[r]
            k = i // 2
            nc.sync.dma_start(
                out=planes[r][i % 2][k : P : 32, :, :].bitcast(I32),
                in_=(W_scales, data_scales)[i % 2][g0:g1, k : 16 : 4, :].rearrange("g q n -> q g n").bitcast(I32),
            )

        def load_scales(r, first_i, end_i):
            for i in range(first_i, end_i):
                load_scale(r, i)

        def load_w(g):
            wc = sb([P, 2, 2 * OUT], U8, "wc%d" % g)
            nc.sync.dma_start(out=wc[:].bitcast(I32), in_=W_words[g : g + 2].rearrange("g p n -> p g n").bitcast(I32))
            w_code[g] = wc[:, 0, :]
            w_code[g + 1] = wc[:, 1, :]

        def load_w_single(g):
            wc = sb([P, 2 * OUT], U8, "wc%d" % g)
            nc.sync.dma_start(out=wc[:].bitcast(I32), in_=W_words[g].bitcast(I32))
            w_code[g] = wc[:]

        def load_d(g):
            d_code[g] = sb([P, 2 * TOKENS], U8, "dc%d" % g)
            nc.sync.dma_start(out=d_code[g][:].bitcast(I32), in_=data_words[g].bitcast(I32))

        def load_passes(g0, g1):
            for g in range(g0, g1):
                if g % 2 == 0:
                    load_w(g)
                for r in range(1, len(SCALE_RUNS)):
                    if SCALE_RUNS[r][0] == g:
                        zero_planes(r)
                        load_scales(r, 0, 8)
                load_d(g)

        load_b(0, nc.sync)
        load_t()
        load_b(1, nc.sync)
        load_b(2, nc.sync)
        zero_planes(0)
        load_scales(0, 0, 4)
        load_b(3, nc.sync)
        load_b(4, nc.sync)
        load_scales(0, 4, 8)
        load_w_single(0)
        load_d(0)
        load_w_single(1)
        load_passes(1, HEAD_PASSES)

        scr = sb([P, 1], F32, "scr")
        nc.scalar.activation(out=scr[:], in_=first[:, 0:1], func=COPY, scale=2.0)
        wps = bank(7, [P, 512], F32, "wps")
        for i in range(N_WARM):
            nc.tensor.matmul(out=wps[:, 0:P], lhsT=first[:], rhs=first[:], start=True, stop=True)

        bT = {}
        tT = {}
        delta = {}

        def turn(dst, src):
            nc.tensor.transpose(out=dst, in_=src, identity=ident[:])

        def turn_b(a):
            ps = bank(a % 3, [P, 512], BF16, "bTp%d" % a)
            for j in range(4):
                turn(ps[:, P * j : P * (j + 1)], b_raw[a][:, P * j : P * (j + 1)])
            bT[a] = sb([P, 512], BF16, "bT%d" % a)
            nc.vector.tensor_copy(out=bT[a][:], in_=ps[:])

        def turn_t(h):
            ps = bank(T_BANK[h], [P, 512], BF16, "tTp%d" % h)
            for j in range(4):
                turn(ps[:, P * j : P * (j + 1)], t_raw[h][:, P * j : P * (j + 1)])
            tT[h] = sb([P, 512], BF16, "tT%d" % h)
            nc.scalar.copy(
                out=tT[h][:].rearrange("r (p j) -> r p j", j=4),
                in_=ps[:].rearrange("r (j p) -> r p j", j=4),
            )

        def product(a):
            ps = bank(PRODUCT_BANK[a], [P, 512], F32, "prod%d" % a)
            nc.tensor.matmul(out=ps[:], lhsT=tT[a // 4][:, P * (a % 4) : P * (a % 4 + 1)], rhs=bT[a][:], start=True, stop=True)
            delta[a] = sb([P, OUT], F32, "delta%d" % a)
            dst = delta[a][:].rearrange("t (p j) -> t p j", j=4)
            src = ps[:].rearrange("t (j p) -> t p j", j=4)
            if a in SCALAR_PRODUCTS:
                nc.scalar.activation(out=dst, in_=src, func=COPY, scale=2.0)
            else:
                nc.vector.tensor_scalar_mul(out=dst, in0=src, scalar1=2.0)

        turn_b(0)
        turn_t(0)
        turn_b(1)
        turn_t(1)
        turn_b(2)
        turn_b(3)
        for a in range(BLOCKS):
            product(a)
            if a + 4 < BLOCKS:
                turn_b(a + 4)

        load_passes(HEAD_PASSES, PASSES)
        acc = {}

        def mm(u, g):
            b, c0, n, bk = UNITS[u]
            if g == 0:
                acc[u] = bank(bk, [P, 512], F32, "acc%d" % u)
            nc.tensor.matmul_mx(
                out=acc[u][:, 0:n],
                lhsT=d_code[g][:, 2 * P * b : 2 * P * (b + 1)].bitcast(FP4),
                lhsT_scale=d_plane[g][:, P * b : P * (b + 1)],
                rhs=w_code[g][:, 2 * c0 : 2 * (c0 + n)].bitcast(FP4),
                rhs_scale=w_plane[g][:, c0 : c0 + n],
                start=(g == 0),
                stop=(g == PASSES - 1),
            )

        def finish(u):
            b, c0, n, bk = UNITS[u]
            res = sb([P, n], F32, "res%d" % u)
            nc.vector.tensor_tensor(out=res[:], in0=acc[u][:, 0:n], in1=delta[b][:, c0 : c0 + n], op=ADD)
            nc.sync.dma_start(out=out[b][:, c0 : c0 + n], in_=res[:])

        for g in range(G1):
            for u in range(8):
                mm(u, g)
        for u in range(8):
            for g in range(G1, PASSES):
                mm(u, g)
            finish(u)
        for g in range(PASSES):
            mm(8, g)
        finish(8)
